import numpy as np
import ml_dtypes


def mxq(x, axis, fmt="e4m3"):
    dtype, down = {"e4m3": (ml_dtypes.float8_e4m3fn, 7), "e5m2": (ml_dtypes.float8_e5m2, 14)}[fmt]
    v = np.moveaxis(np.asarray(x, np.float32).astype(ml_dtypes.bfloat16).astype(np.float64), axis, -1)
    blocks = v.reshape(v.shape[:-1] + (-1, 32))
    amax = np.abs(blocks).max(-1, keepdims=True)
    byte = np.maximum(np.where(amax > 0, np.frexp(amax)[1] - 1 + 127, 0) - down, 1)
    scale = np.exp2(byte - 127.0)
    codes = (blocks / scale).astype(np.float32).astype(dtype).astype(np.float64)
    return np.moveaxis((codes * scale).reshape(v.shape), -1, axis)


WIDE = False


def mx_kscale(k):
    if not WIDE:
        return np.ones(k)
    levels = np.array([30, -30])
    if k % 512:
        return np.exp2(np.random.permutation(np.resize(levels, k // 32))).repeat(32)
    a = np.empty((k // 512, 16))
    for p in range(k // 512):
        a[p, :8] = np.random.permutation(np.resize(levels, 8))
        for g in range(8):
            far = levels[np.abs(levels - a[p, g]) >= 10]
            a[p, g + 8] = far[np.random.randint(len(far))]
    return np.exp2(a.ravel()).repeat(32)


BF16 = ml_dtypes.bfloat16


def bf(x):
    return np.asarray(x, np.float32).astype(BF16)


def f64(x):
    return np.asarray(x).astype(np.float64)


B, S, D, H = 1, 512, 2048, 16
HD = D // H
HALF = HD // 2


def rotary(v, cos, sin):
    p = v.reshape(B, S, H, HALF, 2)
    vr, vi = p[..., 0], p[..., 1]
    c = cos[None, :, None, :]
    s = sin[None, :, None, :]
    return np.stack([vr * c - vi * s, vr * s + vi * c], axis=-1).reshape(B, S, H, HD)


def setup_inputs():
    s = mx_kscale(D)
    inv_freq = 1.0 / (10000.0 ** (np.arange(0, HD, 2) / HD))
    angles = np.arange(S)[:, None] * inv_freq[None, :]
    return {"x": bf(np.random.standard_normal((B, S, D)) * s),
            "freqs_cos": bf(np.cos(angles)), "freqs_sin": bf(np.sin(angles)),
            "wq": bf(np.random.standard_normal((D, D)) * 1.4 / np.sqrt(D) / s[:, None]),
            "wk": bf(np.random.standard_normal((D, D)) * 1.4 / np.sqrt(D) / s[:, None])}


def reference(x, freqs_cos, freqs_sin, wq, wk):
    xq = mxq(f64(x), 2, "e5m2")
    q = (xq @ mxq(f64(wq), 0, "e4m3")).reshape(B, S, H, HD)
    k = (xq @ mxq(f64(wk), 0, "e4m3")).reshape(B, S, H, HD)
    c, s = f64(freqs_cos), f64(freqs_sin)
    return rotary(q, c, s), rotary(k, c, s)

@@ -1,0 +1,223 @@
+from contextlib import ExitStack
+
+import concourse.mybir as mybir
+from concourse.masks import make_identity
+
+S, D = 512, 2048
+HD = 128
+HALF = HD // 2
+FLOPS = 2 * 2 * S * D * D + 3 * 2 * S * D
+
+F32 = mybir.dt.float32
+BF16 = mybir.dt.bfloat16
+U32 = mybir.dt.uint32
+U8 = mybir.dt.uint8
+E4M3X4 = mybir.dt.float8_e4m3fn_x4
+E5M2X4 = mybir.dt.float8_e5m2_x4
+ALU = mybir.AluOpType
+
+P = 128
+PACK = 4
+K_PASS = P * PACK
+PASSES = D // K_PASS
+TOK_TILES = S // P
+N_TILE = 512
+HEADS_PER_BLOCK = N_TILE // HD
+BLOCKS_PER_W = D // N_TILE
+BLOCKS = 2 * BLOCKS_PER_W
+NARROW_BLOCKS = 2
+WIDE = 2 * N_TILE
+HEAD_PIECES = PASSES + 2
+HEAD_VECTOR_COLS = 384
+LOOP_VECTOR_COLS = 320
+
+
+def tile_attention_pa_kernel(tc, x, freqs_cos, freqs_sin, wq, wk, out_0, out_1):
+    nc = tc.nc
+    weights = (wq, wk)
+    x_rows = x.rearrange("b s k -> (b s) k").rearrange("(p m) k -> p m k", m=TOK_TILES)
+    out_rows = [
+        o.rearrange("b s h d -> (b s) (h d)").rearrange("(p m) n -> p m n", m=TOK_TILES) for o in (out_0, out_1)
+    ]
+
+    with ExitStack() as ctx:
+        keep = ctx.enter_context(tc.tile_pool(name="keep", bufs=1))
+        stage = ctx.enter_context(tc.tile_pool(name="stage", bufs=1))
+        psum = ctx.enter_context(tc.psum_pool(name="psum", bufs=1))
+        ctx.enter_context(tc.manual_schedule())
+
+        cos_raw = keep.tile([P, TOK_TILES * HALF], BF16)
+        sin_raw = keep.tile([P, TOK_TILES * HALF], BF16)
+        nc.scalar.dma_start(out=sin_raw[:], in_=freqs_sin.rearrange("(p m) i -> p (m i)", m=TOK_TILES))
+        nc.scalar.dma_start(out=cos_raw[:], in_=freqs_cos.rearrange("(p m) i -> p (m i)", m=TOK_TILES))
+
+        w_raw = {}
+        x_raw = {}
+
+        def load_w(block, g, width):
+            w = weights[block // BLOCKS_PER_W]
+            col = (block % BLOCKS_PER_W) * N_TILE
+            raw = keep.tile([P, PACK, width], BF16, name="w_raw_%d_%d" % (block, g))
+            rows = w[g * K_PASS:(g + 1) * K_PASS, col:col + width]
+            nc.sync.dma_start(out=raw[:], in_=rows.rearrange("(p j) n -> p j n", j=PACK))
+            for i in range(width // N_TILE):
+                w_raw[(block + i, g)] = raw[:, :, i * N_TILE:(i + 1) * N_TILE]
+
+        def load_x(m):
+            raw = keep.tile([P, D], BF16, name="x_raw_%d" % m)
+            nc.sync.dma_start(out=raw[:], in_=x_rows[:, m, :])
+            x_raw[m] = raw
+
+        narrow = [(b, g) for b in range(NARROW_BLOCKS) for g in range(PASSES)]
+        for i, (b, g) in enumerate(narrow):
+            load_w(b, g, N_TILE)
+            if 1 <= i <= TOK_TILES:
+                load_x(i - 1)
+        for b in range(NARROW_BLOCKS, BLOCKS, 2):
+            for g in range(PASSES):
+                load_w(b, g, WIDE)
+
+        ident = keep.tile([P, P], F32)
+        make_identity(nc, ident[:])
+        signs = keep.tile([P, 2], F32)
+        nc.vector.memset(signs[:, 0:1], -1.0)
+        nc.vector.memset(signs[:, 1:2], 1.0)
+        pairs = TOK_TILES * HALF
+        sin_tab = keep.tile([P, pairs, 2], F32)
+        cos_tab = keep.tile([P, pairs, 2], F32)
+        nc.vector.tensor_tensor(
+            out=sin_tab[:],
+            in0=sin_raw[:].unsqueeze(2).to_broadcast([P, pairs, 2]),
+            in1=signs[:].unsqueeze(1).to_broadcast([P, pairs, 2]),
+            op=ALU.mult,
+        )
+        nc.vector.tensor_copy(out=cos_tab[:], in_=cos_raw[:].unsqueeze(2).to_broadcast([P, pairs, 2]))
+
+        grouped = {}
+        w_mx = {}
+        x_mx = {}
+        acc = {}
+
+        def interleave(block, g, vector_cols):
+            tile = stage.tile([P, N_TILE, PACK], BF16, tag="grouped", bufs=5, align_bytes=64)
+            src = w_raw[(block, g)]
+            if vector_cols > 0:
+                nc.vector.tensor_copy(out=tile[:, :vector_cols, :], in_=src[:, :, :vector_cols].rearrange("p j n -> p n j"))
+            if vector_cols < N_TILE:
+                nc.scalar.copy(out=tile[:, vector_cols:, :], in_=src[:, :, vector_cols:].rearrange("p j n -> p n j"))
+            grouped[(block, g)] = tile
+
+        def quantize_w(block, g):
+            codes = stage.tile([P, N_TILE], U32, tag="w_codes", bufs=6, align_bytes=64)
+            scales = stage.tile([P, N_TILE], U8, tag="w_scales", bufs=6, align_bytes=64)
+            nc.vector.quantize_mx(
+                out=codes[:].bitcast(E4M3X4),
+                scales=scales[:],
+                in_=grouped[(block, g)][:].rearrange("p n j -> p (n j)"),
+            )
+            w_mx[(block, g)] = (codes, scales)
+
+        def transpose_x(m):
+            words = x_raw[m][:].bitcast(F32)
+            tile = stage.tile([P, PASSES * P * PACK], BF16, tag="x_grouped", bufs=2, align_bytes=64)
+            tile_words = tile[:].bitcast(F32).rearrange("p (g r u) -> p g r u", g=PASSES, u=2)
+            for half in range(2):
+                bank = psum.tile([P, 2, 2, P], F32, tag="x_bank", bufs=4)
+                for gg in range(2):
+                    g = 2 * half + gg
+                    for u in range(2):
+                        nc.tensor.transpose(bank[:, gg, u, :], words[:, 256 * g + u:256 * (g + 1):2], ident[:])
+                nc.scalar.copy(
+                    out=tile_words[:, 2 * half:2 * half + 2, :, :],
+                    in_=bank[:].rearrange("p g u r -> p g r u"),
+                )
+            grouped[("x", m)] = tile
+
+        def quantize_x(m):
+            codes = keep.tile([P, PASSES * P], U32, name="x_codes_%d" % m, align_bytes=64)
+            scales = keep.tile([P, PASSES * P], U8, name="x_scales_%d" % m, align_bytes=64)
+            nc.vector.quantize_mx(out=codes[:].bitcast(E5M2X4), scales=scales[:], in_=grouped[("x", m)][:])
+            x_mx[m] = (codes, scales)
+
+        def multiply(block, g, m):
+            if g == 0:
+                acc[m] = psum.tile([P, N_TILE], F32, name="acc_%d" % m)
+            x_codes, x_scales = x_mx[m]
+            w_codes, w_scales = w_mx[(block, g)]
+            cols = slice(g * P, (g + 1) * P)
+            nc.tensor.matmul_mx(
+                out=acc[m][:],
+                lhsT=x_codes[:, cols].bitcast(E5M2X4),
+                lhsT_scale=x_scales[:, cols],
+                rhs=w_codes[:].bitcast(E4M3X4),
+                rhs_scale=w_scales[:],
+                start=(g == 0),
+                stop=(g == PASSES - 1),
+            )
+
+        def products(m, res):
+            shape = [P, HEADS_PER_BLOCK, HALF, 2]
+            v = acc[m][:].rearrange("p (h i e) -> p h i e", h=HEADS_PER_BLOCK, e=2)
+            rows = slice(m * HALF, (m + 1) * HALF)
+            nc.vector.tensor_tensor(
+                out=res[:, m, :].rearrange("p (h i e) -> p h i e", h=HEADS_PER_BLOCK, e=2),
+                in0=v,
+                in1=cos_tab[:, rows, :].unsqueeze(1).to_broadcast(shape),
+                op=ALU.mult,
+            )
+            cross = stage.tile([P, N_TILE], F32, tag="cross", bufs=4)
+            nc.vector.tensor_tensor(
+                out=cross[:].rearrange("p (h i e) -> p h i e", h=HEADS_PER_BLOCK, e=2),
+                in0=v[:, :, :, ::-1],
+                in1=sin_tab[:, rows, :].unsqueeze(1).to_broadcast(shape),
+                op=ALU.mult,
+            )
+            return cross
+
+        interleave(*narrow[0], HEAD_VECTOR_COLS)
+        for i in range(1, HEAD_PIECES):
+            interleave(*narrow[i], HEAD_VECTOR_COLS)
+            quantize_w(*narrow[i - 1])
+            if i >= 2:
+                quantize_x(i - 2)
+            if i <= TOK_TILES:
+                transpose_x(i - 1)
+        quantize_w(*narrow[HEAD_PIECES - 1])
+        for m in range(TOK_TILES):
+            for g in range(PASSES):
+                multiply(0, g, m)
+
+        last = TOK_TILES - 1
+        for b in range(BLOCKS):
+            nxt = b + 1
+            out_cols = slice((b % BLOCKS_PER_W) * N_TILE, (b % BLOCKS_PER_W + 1) * N_TILE)
+            dst = out_rows[b // BLOCKS_PER_W]
+            res = stage.tile([P, TOK_TILES, N_TILE], F32, tag="res", bufs=3)
+            for m in range(TOK_TILES):
+                cross = products(m, res)
+                if m < last:
+                    nc.gpsimd.tensor_tensor(out=res[:, m, :], in0=res[:, m, :], in1=cross[:], op=ALU.add)
+                    if nxt == BLOCKS:
+                        nc.sync.dma_start(out=dst[:, m, out_cols], in_=res[:, m, :])
+            if nxt < BLOCKS:
+                interleave(nxt, 2, 0)
+                interleave(nxt, 3, 0)
+                quantize_w(nxt, 2)
+            nc.vector.tensor_tensor(out=res[:, last, :], in0=res[:, last, :], in1=cross[:], op=ALU.add)
+            if nxt == BLOCKS:
+                nc.sync.dma_start(out=dst[:, last, out_cols], in_=res[:, last, :])
+                break
+            nc.sync.dma_start(out=dst[:, :, out_cols], in_=res[:])
+            for m in range(TOK_TILES):
+                multiply(nxt, 0, m)
+                multiply(nxt, 1, m)
+            if nxt + 1 < BLOCKS:
+                interleave(nxt + 1, 0, 0)
+                interleave(nxt + 1, 1, LOOP_VECTOR_COLS)
+            quantize_w(nxt, 3)
+            for g in (2, 3):
+                for m in range(TOK_TILES):
+                    multiply(nxt, g, m)
+            if nxt + 1 < BLOCKS:
+                quantize_w(nxt + 1, 0)
+                quantize_w(nxt + 1, 1)

@@ -25,11 +25,11 @@ N_TILE = 512
 HEADS_PER_BLOCK = N_TILE // HD
 BLOCKS_PER_W = D // N_TILE
 BLOCKS = 2 * BLOCKS_PER_W
-NARROW_BLOCKS = 2
-WIDE = 2 * N_TILE
+RUN = 4
+RAW_BUFS = 24
+EARLY_BLOCKS = 5
 HEAD_PIECES = PASSES + 2
-HEAD_VECTOR_COLS = 384
-LOOP_VECTOR_COLS = 320
+VECTOR_COLS = 384
 
 
 def tile_attention_pa_kernel(tc, x, freqs_cos, freqs_sin, wq, wk, out_0, out_1):
@@ -52,73 +52,76 @@ def tile_attention_pa_kernel(tc, x, freqs_cos, freqs_sin, wq, wk, out_0, out_1):
         nc.scalar.dma_start(out=cos_raw[:], in_=freqs_cos.rearrange("(p m) i -> p (m i)", m=TOK_TILES))
 
         w_raw = {}
-        x_raw = {}
+        x_raw = stage.tile([P, TOK_TILES, D], BF16, tag="prod", bufs=2)
 
-        def load_w(block, g, width):
+        def load_w(block, g):
             w = weights[block // BLOCKS_PER_W]
             col = (block % BLOCKS_PER_W) * N_TILE
-            raw = keep.tile([P, PACK, width], BF16, name="w_raw_%d_%d" % (block, g))
-            rows = w[g * K_PASS:(g + 1) * K_PASS, col:col + width]
+            raw = stage.tile([P, PACK, N_TILE], BF16, tag="w_raw", bufs=RAW_BUFS)
+            rows = w[g * K_PASS:(g + 1) * K_PASS, col:col + N_TILE]
             nc.sync.dma_start(out=raw[:], in_=rows.rearrange("(p j) n -> p j n", j=PACK))
-            for i in range(width // N_TILE):
-                w_raw[(block + i, g)] = raw[:, :, i * N_TILE:(i + 1) * N_TILE]
+            w_raw[(block, g)] = raw
 
-        def load_x(m):
-            raw = keep.tile([P, D], BF16, name="x_raw_%d" % m)
-            nc.sync.dma_start(out=raw[:], in_=x_rows[:, m, :])
-            x_raw[m] = raw
-
-        narrow = [(b, g) for b in range(NARROW_BLOCKS) for g in range(PASSES)]
-        for i, (b, g) in enumerate(narrow):
-            load_w(b, g, N_TILE)
+        pieces = [(b, g) for b in range(BLOCKS) for g in range(PASSES)]
+        for i, (b, g) in enumerate(pieces[:EARLY_BLOCKS * PASSES]):
+            load_w(b, g)
             if 1 <= i <= TOK_TILES:
-                load_x(i - 1)
-        for b in range(NARROW_BLOCKS, BLOCKS, 2):
-            for g in range(PASSES):
-                load_w(b, g, WIDE)
+                nc.sync.dma_start(out=x_raw[:, i - 1, :], in_=x_rows[:, i - 1, :])
 
         ident = keep.tile([P, P], F32)
         make_identity(nc, ident[:])
         signs = keep.tile([P, 2], F32)
-        nc.vector.memset(signs[:, 0:1], -1.0)
-        nc.vector.memset(signs[:, 1:2], 1.0)
-        pairs = TOK_TILES * HALF
-        sin_tab = keep.tile([P, pairs, 2], F32)
-        cos_tab = keep.tile([P, pairs, 2], F32)
+        nc.vector.memset(signs[:, 0:1], 1.0)
+        nc.vector.memset(signs[:, 1:2], -1.0)
+        table = keep.tile([P, TOK_TILES, 2, HALF, 2], F32)
+        half_shape = [P, TOK_TILES, HALF, 2]
         nc.vector.tensor_tensor(
-            out=sin_tab[:],
-            in0=sin_raw[:].unsqueeze(2).to_broadcast([P, pairs, 2]),
-            in1=signs[:].unsqueeze(1).to_broadcast([P, pairs, 2]),
+            out=table[:, :, 1, :, :],
+            in0=sin_raw[:].rearrange("p (m i) -> p m i", m=TOK_TILES).unsqueeze(3).to_broadcast(half_shape),
+            in1=signs[:].unsqueeze(1).unsqueeze(1).to_broadcast(half_shape),
             op=ALU.mult,
         )
-        nc.vector.tensor_copy(out=cos_tab[:], in_=cos_raw[:].unsqueeze(2).to_broadcast([P, pairs, 2]))
+        nc.vector.tensor_copy(
+            out=table[:, :, 0, :, :],
+            in_=cos_raw[:].rearrange("p (m i) -> p m i", m=TOK_TILES).unsqueeze(3).to_broadcast(half_shape),
+        )
 
         grouped = {}
+        x_grouped = {}
         w_mx = {}
         x_mx = {}
         acc = {}
 
-        def interleave(block, g, vector_cols):
-            tile = stage.tile([P, N_TILE, PACK], BF16, tag="grouped", bufs=5, align_bytes=64)
-            src = w_raw[(block, g)]
-            if vector_cols > 0:
-                nc.vector.tensor_copy(out=tile[:, :vector_cols, :], in_=src[:, :, :vector_cols].rearrange("p j n -> p n j"))
-            if vector_cols < N_TILE:
-                nc.scalar.copy(out=tile[:, vector_cols:, :], in_=src[:, :, vector_cols:].rearrange("p j n -> p n j"))
-            grouped[(block, g)] = tile
+        def region(block, g):
+            if g < 2:
+                return "first_%d" % (block % 3)
+            return "second_%d" % (block % 2)
 
-        def quantize_w(block, g):
-            codes = stage.tile([P, N_TILE], U32, tag="w_codes", bufs=6, align_bytes=64)
-            scales = stage.tile([P, N_TILE], U8, tag="w_scales", bufs=6, align_bytes=64)
-            nc.vector.quantize_mx(
-                out=codes[:].bitcast(E4M3X4),
-                scales=scales[:],
-                in_=grouped[(block, g)][:].rearrange("p n j -> p (n j)"),
+        def interleave(copy, block, g, cols):
+            if (block, g // 2) not in grouped:
+                grouped[(block, g // 2)] = stage.tile(
+                    [P, 2, N_TILE, PACK], BF16, name="pair", tag=region(block, g), align_bytes=64
+                )
+            copy(
+                out=grouped[(block, g // 2)][:, g % 2, cols, :].rearrange("p (c i) j -> p c j i", i=RUN),
+                in_=w_raw[(block, g)][:, :, cols].rearrange("p j (c i) -> p c j i", i=RUN),
             )
-            w_mx[(block, g)] = (codes, scales)
+
+        def quantize_w(block, g, count):
+            if g % 2 == 0:
+                codes = stage.tile([P, 2, N_TILE], U32, tag="w_codes", bufs=3, align_bytes=64)
+                scales = stage.tile([P, 2, N_TILE], U8, tag="w_scales", bufs=3, align_bytes=64)
+                w_mx[(block, g // 2)] = (codes, scales)
+            codes, scales = w_mx[(block, g // 2)]
+            passes = slice(g % 2, g % 2 + count)
+            nc.vector.quantize_mx(
+                out=codes[:, passes, :].rearrange("p g n -> p (g n)").bitcast(E4M3X4),
+                scales=scales[:, passes, :].rearrange("p g n -> p (g n)"),
+                in_=grouped[(block, g // 2)][:, passes, :, :].rearrange("p g n j -> p (g n j)"),
+            )
 
         def transpose_x(m):
-            words = x_raw[m][:].bitcast(F32)
+            words = x_raw[:, m, :].bitcast(F32)
             tile = stage.tile([P, PASSES * P * PACK], BF16, tag="x_grouped", bufs=2, align_bytes=64)
             tile_words = tile[:].bitcast(F32).rearrange("p (g r u) -> p g r u", g=PASSES, u=2)
             for half in range(2):
@@ -131,93 +134,105 @@ def tile_attention_pa_kernel(tc, x, freqs_cos, freqs_sin, wq, wk, out_0, out_1):
                     out=tile_words[:, 2 * half:2 * half + 2, :, :],
                     in_=bank[:].rearrange("p g u r -> p g r u"),
                 )
-            grouped[("x", m)] = tile
+            x_grouped[m] = tile
 
         def quantize_x(m):
             codes = keep.tile([P, PASSES * P], U32, name="x_codes_%d" % m, align_bytes=64)
             scales = keep.tile([P, PASSES * P], U8, name="x_scales_%d" % m, align_bytes=64)
-            nc.vector.quantize_mx(out=codes[:].bitcast(E5M2X4), scales=scales[:], in_=grouped[("x", m)][:])
+            nc.vector.quantize_mx(out=codes[:].bitcast(E5M2X4), scales=scales[:], in_=x_grouped[m][:])
             x_mx[m] = (codes, scales)
 
         def multiply(block, g, m):
             if g == 0:
                 acc[m] = psum.tile([P, N_TILE], F32, name="acc_%d" % m)
             x_codes, x_scales = x_mx[m]
-            w_codes, w_scales = w_mx[(block, g)]
+            w_codes, w_scales = w_mx[(block, g // 2)]
             cols = slice(g * P, (g + 1) * P)
             nc.tensor.matmul_mx(
                 out=acc[m][:],
                 lhsT=x_codes[:, cols].bitcast(E5M2X4),
                 lhsT_scale=x_scales[:, cols],
-                rhs=w_codes[:].bitcast(E4M3X4),
-                rhs_scale=w_scales[:],
+                rhs=w_codes[:, g % 2, :].bitcast(E4M3X4),
+                rhs_scale=w_scales[:, g % 2, :],
                 start=(g == 0),
                 stop=(g == PASSES - 1),
             )
 
-        def products(m, res):
-            shape = [P, HEADS_PER_BLOCK, HALF, 2]
-            v = acc[m][:].rearrange("p (h i e) -> p h i e", h=HEADS_PER_BLOCK, e=2)
-            rows = slice(m * HALF, (m + 1) * HALF)
+        def products(m, prod):
+            shape = [P, 2, HEADS_PER_BLOCK, HD]
             nc.vector.tensor_tensor(
-                out=res[:, m, :].rearrange("p (h i e) -> p h i e", h=HEADS_PER_BLOCK, e=2),
-                in0=v,
-                in1=cos_tab[:, rows, :].unsqueeze(1).to_broadcast(shape),
+                out=prod[:, m, :, :].rearrange("p a (h d) -> p a h d", h=HEADS_PER_BLOCK),
+                in0=acc[m][:].rearrange("p (h d) -> p h d", h=HEADS_PER_BLOCK).unsqueeze(1).to_broadcast(shape),
+                in1=table[:, m, :, :, :].rearrange("p a i e -> p a (i e)").unsqueeze(2).to_broadcast(shape),
                 op=ALU.mult,
             )
-            cross = stage.tile([P, N_TILE], F32, tag="cross", bufs=4)
-            nc.vector.tensor_tensor(
-                out=cross[:].rearrange("p (h i e) -> p h i e", h=HEADS_PER_BLOCK, e=2),
-                in0=v[:, :, :, ::-1],
-                in1=sin_tab[:, rows, :].unsqueeze(1).to_broadcast(shape),
-                op=ALU.mult,
-            )
-            return cross
 
-        interleave(*narrow[0], HEAD_VECTOR_COLS)
-        for i in range(1, HEAD_PIECES):
-            interleave(*narrow[i], HEAD_VECTOR_COLS)
-            quantize_w(*narrow[i - 1])
+        def add_and_store(engine, block, prod, res, tiles):
+            engine.tensor_tensor(
+                out=res[:, tiles, :].rearrange("p m (j e) -> p m j e", e=2),
+                in0=prod[:, tiles, 0, :].rearrange("p m (j e) -> p m j e", e=2),
+                in1=prod[:, tiles, 1, :].rearrange("p m (j e) -> p m j e", e=2)[:, :, :, ::-1],
+                op=ALU.add,
+            )
+            col = (block % BLOCKS_PER_W) * N_TILE
+            nc.sync.dma_start(out=out_rows[block // BLOCKS_PER_W][:, tiles, col:col + N_TILE], in_=res[:, tiles, :])
+
+        def result_tile(tag):
+            res = stage.tile([P, TOK_TILES, N_TILE], F32, tag=tag, align_bytes=64)
+            return res
+
+        on_vector, on_scalar = nc.vector.tensor_copy, nc.scalar.copy
+        whole, vector_part, scalar_part = slice(0, N_TILE), slice(0, VECTOR_COLS), slice(VECTOR_COLS, N_TILE)
+        last = BLOCKS - 1
+
+        for i in range(HEAD_PIECES):
+            interleave(on_vector, *pieces[i], vector_part)
+            interleave(on_scalar, *pieces[i], scalar_part)
+            if i >= 1:
+                quantize_w(*pieces[i - 1], 1)
             if i >= 2:
                 quantize_x(i - 2)
-            if i <= TOK_TILES:
+            if 1 <= i <= TOK_TILES:
                 transpose_x(i - 1)
-        quantize_w(*narrow[HEAD_PIECES - 1])
+        quantize_w(*pieces[HEAD_PIECES - 1], 1)
+        interleave(on_vector, 1, 2, vector_part)
         for m in range(TOK_TILES):
             for g in range(PASSES):
                 multiply(0, g, m)
 
-        last = TOK_TILES - 1
+        prods = {}
         for b in range(BLOCKS):
             nxt = b + 1
-            out_cols = slice((b % BLOCKS_PER_W) * N_TILE, (b % BLOCKS_PER_W + 1) * N_TILE)
-            dst = out_rows[b // BLOCKS_PER_W]
-            res = stage.tile([P, TOK_TILES, N_TILE], F32, tag="res", bufs=3)
+            prods[b] = stage.tile([P, TOK_TILES, 2, N_TILE], F32, name="prod", tag="prod", bufs=2)
+            if b == last:
+                add_and_store(nc.vector, b - 1, prods[b - 1], result_tile(region(nxt, 0)), slice(2, 4))
+                add_and_store(nc.gpsimd, b - 1, prods[b - 1], result_tile(region(b, 2)), slice(0, 2))
+            elif b > 0:
+                add_and_store(nc.gpsimd, b - 1, prods[b - 1], result_tile(region(nxt, 0)), slice(0, TOK_TILES))
+                if EARLY_BLOCKS + b - 1 < BLOCKS:
+                    for g in range(PASSES):
+                        load_w(EARLY_BLOCKS + b - 1, g)
             for m in range(TOK_TILES):
-                cross = products(m, res)
-                if m < last:
-                    nc.gpsimd.tensor_tensor(out=res[:, m, :], in0=res[:, m, :], in1=cross[:], op=ALU.add)
-                    if nxt == BLOCKS:
-                        nc.sync.dma_start(out=dst[:, m, out_cols], in_=res[:, m, :])
-            if nxt < BLOCKS:
-                interleave(nxt, 2, 0)
-                interleave(nxt, 3, 0)
-                quantize_w(nxt, 2)
-            nc.vector.tensor_tensor(out=res[:, last, :], in0=res[:, last, :], in1=cross[:], op=ALU.add)
-            if nxt == BLOCKS:
-                nc.sync.dma_start(out=dst[:, last, out_cols], in_=res[:, last, :])
+                products(m, prods[b])
+            if b == last:
                 break
-            nc.sync.dma_start(out=dst[:, :, out_cols], in_=res[:])
             for m in range(TOK_TILES):
                 multiply(nxt, 0, m)
                 multiply(nxt, 1, m)
-            if nxt + 1 < BLOCKS:
-                interleave(nxt + 1, 0, 0)
-                interleave(nxt + 1, 1, LOOP_VECTOR_COLS)
-            quantize_w(nxt, 3)
-            for g in (2, 3):
-                for m in range(TOK_TILES):
-                    multiply(nxt, g, m)
-            if nxt + 1 < BLOCKS:
-                quantize_w(nxt + 1, 0)
-                quantize_w(nxt + 1, 1)
+            interleave(on_scalar, nxt, 2, scalar_part if nxt < last else whole)
+            interleave(on_scalar, nxt, 3, whole)
+            if nxt < last:
+                interleave(on_scalar, nxt + 1, 0, whole)
+                interleave(on_scalar, nxt + 1, 1, whole)
+            quantize_w(nxt, 2, 2)
+            for m in range(TOK_TILES):
+                multiply(nxt, 2, m)
+                multiply(nxt, 3, m)
+            if nxt < last:
+                quantize_w(nxt + 1, 0, 2)
+            if nxt + 1 < last:
+                interleave(on_vector, nxt + 1, 2, vector_part)
+
+        res = result_tile(region(BLOCKS + 1, 0))
+        for m in range(TOK_TILES):
+            add_and_store(nc.gpsimd if m == 0 else nc.vector, last, prods[last], res, slice(m, m + 1))

@@ -29,7 +29,8 @@ RUN = 4
 RAW_BUFS = 24
 EARLY_BLOCKS = 5
 HEAD_PIECES = PASSES + 2
-VECTOR_COLS = 384
+HEAD_VECTOR_COLS = 384
+LOOP_VECTOR_COLS = 320
 
 
 def tile_attention_pa_kernel(tc, x, freqs_cos, freqs_sin, wq, wk, out_0, out_1):
@@ -182,12 +183,14 @@ def tile_attention_pa_kernel(tc, x, freqs_cos, freqs_sin, wq, wk, out_0, out_1):
             return res
 
         on_vector, on_scalar = nc.vector.tensor_copy, nc.scalar.copy
-        whole, vector_part, scalar_part = slice(0, N_TILE), slice(0, VECTOR_COLS), slice(VECTOR_COLS, N_TILE)
+        whole = slice(0, N_TILE)
+        vector_part, scalar_part = slice(0, LOOP_VECTOR_COLS), slice(LOOP_VECTOR_COLS, N_TILE)
+        swapped = [m ^ 1 for m in range(TOK_TILES)]
         last = BLOCKS - 1
 
         for i in range(HEAD_PIECES):
-            interleave(on_vector, *pieces[i], vector_part)
-            interleave(on_scalar, *pieces[i], scalar_part)
+            interleave(on_vector, *pieces[i], slice(0, HEAD_VECTOR_COLS))
+            interleave(on_scalar, *pieces[i], slice(HEAD_VECTOR_COLS, N_TILE))
             if i >= 1:
                 quantize_w(*pieces[i - 1], 1)
             if i >= 2:
@@ -196,7 +199,7 @@ def tile_attention_pa_kernel(tc, x, freqs_cos, freqs_sin, wq, wk, out_0, out_1):
                 transpose_x(i - 1)
         quantize_w(*pieces[HEAD_PIECES - 1], 1)
         interleave(on_vector, 1, 2, vector_part)
-        for m in range(TOK_TILES):
+        for m in swapped:
             for g in range(PASSES):
                 multiply(0, g, m)
 
@@ -225,7 +228,7 @@ def tile_attention_pa_kernel(tc, x, freqs_cos, freqs_sin, wq, wk, out_0, out_1):
                 interleave(on_scalar, nxt + 1, 0, whole)
                 interleave(on_scalar, nxt + 1, 1, whole)
             quantize_w(nxt, 2, 2)
-            for m in range(TOK_TILES):
+            for m in swapped if nxt + 1 < last else range(TOK_TILES):
                 multiply(nxt, 2, m)
                 multiply(nxt, 3, m)
             if nxt < last:

from contextlib import ExitStack

import concourse.mybir as mybir
from concourse.masks import make_identity

S, D = 512, 2048
HD = 128
HALF = HD // 2
FLOPS = 2 * 2 * S * D * D + 3 * 2 * S * D

F32 = mybir.dt.float32
BF16 = mybir.dt.bfloat16
U32 = mybir.dt.uint32
U8 = mybir.dt.uint8
E4M3X4 = mybir.dt.float8_e4m3fn_x4
E5M2X4 = mybir.dt.float8_e5m2_x4
ALU = mybir.AluOpType

P = 128
PACK = 4
K_PASS = P * PACK
PASSES = D // K_PASS
TOK_TILES = S // P
N_TILE = 512
HEADS_PER_BLOCK = N_TILE // HD
BLOCKS_PER_W = D // N_TILE
BLOCKS = 2 * BLOCKS_PER_W
RUN = 4
RAW_BUFS = 24
EARLY_BLOCKS = 5
HEAD_PIECES = PASSES + 2
HEAD_VECTOR_COLS = 384
LOOP_VECTOR_COLS = 320


def tile_attention_pa_kernel(tc, x, freqs_cos, freqs_sin, wq, wk, out_0, out_1):
    nc = tc.nc
    weights = (wq, wk)
    x_rows = x.rearrange("b s k -> (b s) k").rearrange("(p m) k -> p m k", m=TOK_TILES)
    out_rows = [
        o.rearrange("b s h d -> (b s) (h d)").rearrange("(p m) n -> p m n", m=TOK_TILES) for o in (out_0, out_1)
    ]

    with ExitStack() as ctx:
        keep = ctx.enter_context(tc.tile_pool(name="keep", bufs=1))
        stage = ctx.enter_context(tc.tile_pool(name="stage", bufs=1))
        psum = ctx.enter_context(tc.psum_pool(name="psum", bufs=1))
        ctx.enter_context(tc.manual_schedule())

        cos_raw = keep.tile([P, TOK_TILES * HALF], BF16)
        sin_raw = keep.tile([P, TOK_TILES * HALF], BF16)
        nc.scalar.dma_start(out=sin_raw[:], in_=freqs_sin.rearrange("(p m) i -> p (m i)", m=TOK_TILES))
        nc.scalar.dma_start(out=cos_raw[:], in_=freqs_cos.rearrange("(p m) i -> p (m i)", m=TOK_TILES))

        w_raw = {}
        x_raw = stage.tile([P, TOK_TILES, D], BF16, tag="prod", bufs=2)

        def load_w(block, g):
            w = weights[block // BLOCKS_PER_W]
            col = (block % BLOCKS_PER_W) * N_TILE
            raw = stage.tile([P, PACK, N_TILE], BF16, tag="w_raw", bufs=RAW_BUFS)
            rows = w[g * K_PASS:(g + 1) * K_PASS, col:col + N_TILE]
            nc.sync.dma_start(out=raw[:], in_=rows.rearrange("(p j) n -> p j n", j=PACK))
            w_raw[(block, g)] = raw

        pieces = [(b, g) for b in range(BLOCKS) for g in range(PASSES)]
        for i, (b, g) in enumerate(pieces[:EARLY_BLOCKS * PASSES]):
            load_w(b, g)
            if 1 <= i <= TOK_TILES:
                nc.sync.dma_start(out=x_raw[:, i - 1, :], in_=x_rows[:, i - 1, :])

        ident = keep.tile([P, P], F32)
        make_identity(nc, ident[:])
        signs = keep.tile([P, 2], F32)
        nc.vector.memset(signs[:, 0:1], 1.0)
        nc.vector.memset(signs[:, 1:2], -1.0)
        table = keep.tile([P, TOK_TILES, 2, HALF, 2], F32)
        half_shape = [P, TOK_TILES, HALF, 2]
        nc.vector.tensor_tensor(
            out=table[:, :, 1, :, :],
            in0=sin_raw[:].rearrange("p (m i) -> p m i", m=TOK_TILES).unsqueeze(3).to_broadcast(half_shape),
            in1=signs[:].unsqueeze(1).unsqueeze(1).to_broadcast(half_shape),
            op=ALU.mult,
        )
        nc.vector.tensor_copy(
            out=table[:, :, 0, :, :],
            in_=cos_raw[:].rearrange("p (m i) -> p m i", m=TOK_TILES).unsqueeze(3).to_broadcast(half_shape),
        )

        grouped = {}
        x_grouped = {}
        w_mx = {}
        x_mx = {}
        acc = {}

        def region(block, g):
            if g < 2:
                return "first_%d" % (block % 3)
            return "second_%d" % (block % 2)

        def interleave(copy, block, g, cols):
            if (block, g // 2) not in grouped:
                grouped[(block, g // 2)] = stage.tile(
                    [P, 2, N_TILE, PACK], BF16, name="pair", tag=region(block, g), align_bytes=64
                )
            copy(
                out=grouped[(block, g // 2)][:, g % 2, cols, :].rearrange("p (c i) j -> p c j i", i=RUN),
                in_=w_raw[(block, g)][:, :, cols].rearrange("p j (c i) -> p c j i", i=RUN),
            )

        def quantize_w(block, g, count):
            if g % 2 == 0:
                codes = stage.tile([P, 2, N_TILE], U32, tag="w_codes", bufs=3, align_bytes=64)
                scales = stage.tile([P, 2, N_TILE], U8, tag="w_scales", bufs=3, align_bytes=64)
                w_mx[(block, g // 2)] = (codes, scales)
            codes, scales = w_mx[(block, g // 2)]
            passes = slice(g % 2, g % 2 + count)
            nc.vector.quantize_mx(
                out=codes[:, passes, :].rearrange("p g n -> p (g n)").bitcast(E4M3X4),
                scales=scales[:, passes, :].rearrange("p g n -> p (g n)"),
                in_=grouped[(block, g // 2)][:, passes, :, :].rearrange("p g n j -> p (g n j)"),
            )

        def transpose_x(m):
            words = x_raw[:, m, :].bitcast(F32)
            tile = stage.tile([P, PASSES * P * PACK], BF16, tag="x_grouped", bufs=2, align_bytes=64)
            tile_words = tile[:].bitcast(F32).rearrange("p (g r u) -> p g r u", g=PASSES, u=2)
            for half in range(2):
                bank = psum.tile([P, 2, 2, P], F32, tag="x_bank", bufs=4)
                for gg in range(2):
                    g = 2 * half + gg
                    for u in range(2):
                        nc.tensor.transpose(bank[:, gg, u, :], words[:, 256 * g + u:256 * (g + 1):2], ident[:])
                nc.scalar.copy(
                    out=tile_words[:, 2 * half:2 * half + 2, :, :],
                    in_=bank[:].rearrange("p g u r -> p g r u"),
                )
            x_grouped[m] = tile

        def quantize_x(m):
            codes = keep.tile([P, PASSES * P], U32, name="x_codes_%d" % m, align_bytes=64)
            scales = keep.tile([P, PASSES * P], U8, name="x_scales_%d" % m, align_bytes=64)
            nc.vector.quantize_mx(out=codes[:].bitcast(E5M2X4), scales=scales[:], in_=x_grouped[m][:])
            x_mx[m] = (codes, scales)

        def multiply(block, g, m):
            if g == 0:
                acc[m] = psum.tile([P, N_TILE], F32, name="acc_%d" % m)
            x_codes, x_scales = x_mx[m]
            w_codes, w_scales = w_mx[(block, g // 2)]
            cols = slice(g * P, (g + 1) * P)
            nc.tensor.matmul_mx(
                out=acc[m][:],
                lhsT=x_codes[:, cols].bitcast(E5M2X4),
                lhsT_scale=x_scales[:, cols],
                rhs=w_codes[:, g % 2, :].bitcast(E4M3X4),
                rhs_scale=w_scales[:, g % 2, :],
                start=(g == 0),
                stop=(g == PASSES - 1),
            )

        def products(m, prod):
            shape = [P, 2, HEADS_PER_BLOCK, HD]
            nc.vector.tensor_tensor(
                out=prod[:, m, :, :].rearrange("p a (h d) -> p a h d", h=HEADS_PER_BLOCK),
                in0=acc[m][:].rearrange("p (h d) -> p h d", h=HEADS_PER_BLOCK).unsqueeze(1).to_broadcast(shape),
                in1=table[:, m, :, :, :].rearrange("p a i e -> p a (i e)").unsqueeze(2).to_broadcast(shape),
                op=ALU.mult,
            )

        def add_and_store(engine, block, prod, res, tiles):
            engine.tensor_tensor(
                out=res[:, tiles, :].rearrange("p m (j e) -> p m j e", e=2),
                in0=prod[:, tiles, 0, :].rearrange("p m (j e) -> p m j e", e=2),
                in1=prod[:, tiles, 1, :].rearrange("p m (j e) -> p m j e", e=2)[:, :, :, ::-1],
                op=ALU.add,
            )
            col = (block % BLOCKS_PER_W) * N_TILE
            nc.sync.dma_start(out=out_rows[block // BLOCKS_PER_W][:, tiles, col:col + N_TILE], in_=res[:, tiles, :])

        def result_tile(tag):
            res = stage.tile([P, TOK_TILES, N_TILE], F32, tag=tag, align_bytes=64)
            return res

        on_vector, on_scalar = nc.vector.tensor_copy, nc.scalar.copy
        whole = slice(0, N_TILE)
        vector_part, scalar_part = slice(0, LOOP_VECTOR_COLS), slice(LOOP_VECTOR_COLS, N_TILE)
        swapped = [m ^ 1 for m in range(TOK_TILES)]
        last = BLOCKS - 1

        for i in range(HEAD_PIECES):
            interleave(on_vector, *pieces[i], slice(0, HEAD_VECTOR_COLS))
            interleave(on_scalar, *pieces[i], slice(HEAD_VECTOR_COLS, N_TILE))
            if i >= 1:
                quantize_w(*pieces[i - 1], 1)
            if i >= 2:
                quantize_x(i - 2)
            if 1 <= i <= TOK_TILES:
                transpose_x(i - 1)
        quantize_w(*pieces[HEAD_PIECES - 1], 1)
        interleave(on_vector, 1, 2, vector_part)
        for m in swapped:
            for g in range(PASSES):
                multiply(0, g, m)

        prods = {}
        for b in range(BLOCKS):
            nxt = b + 1
            prods[b] = stage.tile([P, TOK_TILES, 2, N_TILE], F32, name="prod", tag="prod", bufs=2)
            if b == last:
                add_and_store(nc.vector, b - 1, prods[b - 1], result_tile(region(nxt, 0)), slice(2, 4))
                add_and_store(nc.gpsimd, b - 1, prods[b - 1], result_tile(region(b, 2)), slice(0, 2))
            elif b > 0:
                add_and_store(nc.gpsimd, b - 1, prods[b - 1], result_tile(region(nxt, 0)), slice(0, TOK_TILES))
                if EARLY_BLOCKS + b - 1 < BLOCKS:
                    for g in range(PASSES):
                        load_w(EARLY_BLOCKS + b - 1, g)
            for m in range(TOK_TILES):
                products(m, prods[b])
            if b == last:
                break
            for m in range(TOK_TILES):
                multiply(nxt, 0, m)
                multiply(nxt, 1, m)
            interleave(on_scalar, nxt, 2, scalar_part if nxt < last else whole)
            interleave(on_scalar, nxt, 3, whole)
            if nxt < last:
                interleave(on_scalar, nxt + 1, 0, whole)
                interleave(on_scalar, nxt + 1, 1, whole)
            quantize_w(nxt, 2, 2)
            for m in swapped if nxt + 1 < last else range(TOK_TILES):
                multiply(nxt, 2, m)
                multiply(nxt, 3, m)
            if nxt < last:
                quantize_w(nxt + 1, 0, 2)
            if nxt + 1 < last:
                interleave(on_vector, nxt + 1, 2, vector_part)

        res = result_tile(region(BLOCKS + 1, 0))
        for m in range(TOK_TILES):
            add_and_store(nc.gpsimd if m == 0 else nc.vector, last, prods[last], res, slice(m, m + 1))
